import numpy as np
import ml_dtypes


def mxq(x, axis, fmt="e4m3"):
    dtype, down = {"e4m3": (ml_dtypes.float8_e4m3fn, 7), "e5m2": (ml_dtypes.float8_e5m2, 14)}[fmt]
    v = np.moveaxis(np.asarray(x, np.float32).astype(ml_dtypes.bfloat16).astype(np.float64), axis, -1)
    blocks = v.reshape(v.shape[:-1] + (-1, 32))
    amax = np.abs(blocks).max(-1, keepdims=True)
    byte = np.maximum(np.where(amax > 0, np.frexp(amax)[1] - 1 + 127, 0) - down, 1)
    scale = np.exp2(byte - 127.0)
    codes = (blocks / scale).astype(np.float32).astype(dtype).astype(np.float64)
    return np.moveaxis((codes * scale).reshape(v.shape), -1, axis)


WIDE = False


def mx_kscale(k):
    if not WIDE:
        return np.ones(k)
    levels = np.array([20, -20, 10, -10, 0])
    a = np.random.permutation(np.resize(levels, k // 512 * 4)).reshape(k // 512, 4)
    idx = np.arange(k)
    return np.exp2(a[idx // 512, idx % 128 // 32])


BF16 = ml_dtypes.bfloat16


def bf(x):
    return np.asarray(x, np.float32).astype(BF16)


def f64(x):
    return np.asarray(x).astype(np.float64)


BLOCK = 128
G, T, K, N = 2, 512, 3584, 1024


def w_eff_of(weight, scale):
    g, n, k = weight.shape
    nb, kb = n // BLOCK, k // BLOCK
    return (weight.reshape(g, nb, BLOCK, kb, BLOCK) * scale[:, :, None, :, None]).reshape(g, n, k)


def setup_inputs():
    u = mx_kscale(N)
    xs = np.random.standard_normal((G, T, K))
    weight = np.random.standard_normal((G, N, K)) / u[None, :, None]
    scale = np.random.uniform(0.5, 1.5, (G, N // BLOCK, K // BLOCK)) * 0.012
    bias = np.random.standard_normal((G, N)) * 0.3
    g = np.random.standard_normal((G, T, N)) * np.exp2(np.random.randint(-12, 1, (G, T, 1))) * 32.0 * u[None, None, :]
    return {"xs": bf(xs), "weight": bf(weight), "scale": bf(scale), "bias": bf(bias), "grad_out": bf(g)}


def reference(xs, weight, scale, bias, grad_out):
    weight, scale, go = f64(weight), f64(scale), f64(grad_out)
    w_eff = w_eff_of(weight, scale)
    return mxq(go, 2, "e5m2") @ mxq(w_eff, 1, "e4m3")

@@ -1,0 +1,250 @@
+from contextlib import ExitStack
+
+import concourse.bass as bass
+import concourse.mybir as mybir
+import concourse.tile as tile
+from concourse.masks import make_identity
+
+G, T, K, N = 2, 512, 3584, 1024
+FLOPS = 2 * G * T * K * N
+BYTES = G * N * K * 2 + G * 8 * 28 * 2 + G * T * N * 2 + G * T * K * 4
+
+BF16 = mybir.dt.bfloat16
+F32 = mybir.dt.float32
+U32 = mybir.dt.uint32
+U8 = mybir.dt.uint8
+E4X4 = mybir.dt.float8_e4m3fn_x4
+E5X4 = mybir.dt.float8_e5m2_x4
+
+P = 128
+KT = 512
+BLK = 128
+NKB = K // BLK
+
+PIN = True
+LOAD_CHUNKS = (((0, 1), (1, 2), (3, 4)), ((0, 4), (4, 3)))
+STORE_CHUNKS = (((0, 3), (3, 4)), ((0, 4), (4, 2), (6, 1)))
+KMAJOR_FROM = 3
+RAW_BUFS = 4
+STAGE_BUFS = 4
+CODE_BUFS = 12
+GRP_BUFS = 3
+S_JOBS = ()
+LOOK = 3
+GRAD_POS = (3, 6)
+GQ0_AT = 5
+
+
+def tile_groupcolumnparallellineardeepseekv3_kernel(tc, xs, weight, scale, bias, grad_out, out):
+    nc = tc.nc
+    mult = mybir.AluOpType.mult
+    copy_fn = mybir.ActivationFunctionType.Copy
+
+    with ExitStack() as ctx:
+        const = ctx.enter_context(tc.tile_pool(name="const", bufs=1))
+        graw_pool = ctx.enter_context(tc.tile_pool(name="graw", bufs=2))
+        ggrp_pool = ctx.enter_context(tc.tile_pool(name="ggrp", bufs=2))
+        raw_pool = ctx.enter_context(tc.tile_pool(name="raw", bufs=RAW_BUFS))
+        grp_pool = ctx.enter_context(tc.tile_pool(name="grp", bufs=GRP_BUFS))
+        grps_pool = ctx.enter_context(tc.tile_pool(name="grps", bufs=2))
+        code_pool = ctx.enter_context(tc.tile_pool(name="code", bufs=CODE_BUFS))
+        stage_pool = ctx.enter_context(tc.tile_pool(name="stage", bufs=STAGE_BUFS))
+        psum = ctx.enter_context(tc.psum_pool(name="psum", bufs=8))
+        if PIN:
+            ctx.enter_context(tc.manual_schedule())
+
+        s_bf = const.tile([P, 4, NKB], BF16, name="s_bf", tag="s_bf")
+        sview = scale.rearrange("g (c q) k -> (g c) q k", q=4)
+        for q in range(4):
+            nc.scalar.dma_start(out=s_bf[32 * q:32 * q + 32, :, :], in_=sview[:, q, :].partition_broadcast(32))
+        s_tab = const.tile([P, 4 * NKB], F32, name="s_tab", tag="s_tab")
+        ident = const.tile([P, P], F32, name="ident", tag="ident")
+        make_identity(nc, ident[:])
+
+        gq = []
+        gs = []
+        for g in range(G):
+            gq_t = const.tile([P, 2, T], U32, name="gq%d" % g, tag="gq%d" % g, align_bytes=64)
+            gs_t = const.tile([P, 2, T], U8, name="gs%d" % g, tag="gs%d" % g, align_bytes=64)
+            gq.append(gq_t)
+            gs.append(gs_t)
+
+        ltiles = []
+        steps = []
+        for g in range(G):
+            for ci, (k0, n) in enumerate(LOAD_CHUNKS[g]):
+                chunk_no = len(ltiles) // 2
+                for c in range(2):
+                    ltiles.append((g, ci, c))
+                if chunk_no >= KMAJOR_FROM:
+                    for kt in range(k0, k0 + n):
+                        for c in range(2):
+                            steps.append((g, ci, c, kt))
+                else:
+                    for c in range(2):
+                        for kt in range(k0, k0 + n):
+                            steps.append((g, ci, c, kt))
+        last_step = {}
+        for si, (g, ci, c, kt) in enumerate(steps):
+            last_step[(g, ci, c)] = si
+        sch_of = {}
+        for g in range(G):
+            for (k0, n) in STORE_CHUNKS[g]:
+                for kt in range(k0, k0 + n):
+                    sch_of[(g, kt)] = (k0, n)
+
+        raw = {}
+        released = {}
+        graw = {}
+        ggrp = {}
+        grad_ready = {}
+        grouped = {}
+        codes = {}
+        stage = {}
+        pend_out = []
+        n_loaded = [0]
+
+        def issue_loads():
+            while n_loaded[0] < len(ltiles):
+                i = n_loaded[0]
+                if i >= RAW_BUFS and ltiles[i - RAW_BUFS] not in released:
+                    return
+                for g in range(G):
+                    if GRAD_POS[g] == i:
+                        gr = graw_pool.tile([P, 4 * N], BF16, name="graw", tag="graw")
+                        nc.sync.dma_start(out=gr[:], in_=grad_out[g].rearrange("(p t) n -> p (t n)", t=4))
+                        graw[g] = gr
+                g, ci, c = ltiles[i]
+                k0, n = LOAD_CHUNKS[g][ci]
+                w = n * KT
+                rt = raw_pool.tile([P, 4, w], BF16, name="raw", tag="raw")
+                nc.sync.dma_start(
+                    out=rt[:],
+                    in_=weight[g, 512 * c:512 * (c + 1), k0 * KT:k0 * KT + w].rearrange("(p j) k -> p j k", j=4),
+                )
+                raw[ltiles[i]] = rt
+                n_loaded[0] += 1
+
+        def grad_transposes(g):
+            g32 = graw[g][:].bitcast(F32)
+            for c in range(2):
+                gg = ggrp_pool.tile([P, 4 * T], BF16, name="ggrp", tag="ggrp", align_bytes=64)
+                ggrp[(g, c)] = gg
+                gg32 = gg[:].bitcast(F32)
+                for tp in range(2):
+                    ps = psum.tile([P, KT], F32, name="ps", tag="ps")
+                    for u in range(2):
+                        for tl in range(2):
+                            base = (2 * tp + tl) * 512 + 256 * c
+                            nc.tensor.transpose(
+                                out=ps[:, u * 256 + tl * 128:u * 256 + tl * 128 + 128],
+                                in_=g32[:, base + u:base + 256:2],
+                                identity=ident[:],
+                            )
+                    nc.scalar.copy(
+                        out=gg32[:, tp * 512:tp * 512 + 512].rearrange("p (x u) -> p x u", u=2),
+                        in_=ps[:].rearrange("p (u x) -> p x u", u=2),
+                    )
+
+        def grad_quantise(g):
+            for c in range(2):
+                nc.vector.quantize_mx(
+                    out=gq[g][:, c, :].bitcast(E5X4),
+                    scales=gs[g][:, c, :],
+                    in_=ggrp[(g, c)][:],
+                )
+            grad_ready[g] = True
+
+        def regroup(si, on_scalar):
+            g, ci, c, kt = steps[si]
+            k0, n = LOAD_CHUNKS[g][ci]
+            rt = raw[(g, ci, c)]
+            if on_scalar:
+                gt = grps_pool.tile([P, KT, 4], BF16, name="grps", tag="grps", align_bytes=64)
+            else:
+                gt = grp_pool.tile([P, KT, 4], BF16, name="grp", tag="grp", align_bytes=64)
+            grouped[si] = gt
+            for b in range(4):
+                x = (kt - k0) * KT + b * BLK
+                col = (2 * g + c) * NKB + 4 * kt + b
+                src = rt[:, :, x:x + BLK].rearrange("p t (c i) -> p c t i", i=4)
+                dst = gt[:, b * BLK:(b + 1) * BLK, :].rearrange("p (c i) t -> p c t i", i=4)
+                if on_scalar:
+                    nc.scalar.activation(out=dst, in_=src, func=copy_fn, scale=s_tab[:, col:col + 1])
+                else:
+                    nc.vector.tensor_scalar(out=dst, in0=src, scalar1=s_tab[:, col:col + 1], scalar2=None, op0=mult)
+
+        def outputs(g, kt):
+            k0, n = sch_of[(g, kt)]
+            groups = ((0, 1), (2, 3)) if n > 2 else ((0, 1, 2, 3),)
+            for tts in groups:
+                if (g, k0, tts[0]) not in stage:
+                    st = stage_pool.tile([P, len(tts), n * KT], F32, name="st", tag="st")
+                    stage[(g, k0, tts[0])] = st
+            for tts in groups:
+                st = stage[(g, k0, tts[0])]
+                for tl, tt in enumerate(tts):
+                    ps = psum.tile([P, KT], F32, name="ps", tag="ps")
+                    for c in range(2):
+                        wq, ws = codes[(g, c, kt)]
+                        nc.tensor.matmul_mx(
+                            out=ps[:],
+                            lhsT=gq[g][:, c, tt * P:(tt + 1) * P].bitcast(E5X4),
+                            lhsT_scale=gs[g][:, c, tt * P:(tt + 1) * P],
+                            rhs=wq[:].bitcast(E4X4),
+                            rhs_scale=ws[:],
+                            start=(c == 0),
+                            stop=(c == 1),
+                        )
+                    nc.scalar.copy(out=st[:, tl, (kt - k0) * KT:(kt - k0 + 1) * KT], in_=ps[:])
+            if kt == k0 + n - 1:
+                oview = out[g].rearrange("(p t) k -> p t k", t=4)
+                for tts in groups:
+                    st = stage[(g, k0, tts[0])]
+                    nc.sync.dma_start(
+                        out=oview[:, tts[0]:tts[0] + len(tts), k0 * KT:(k0 + n) * KT],
+                        in_=st[:],
+                    )
+
+        def quantise(si):
+            g, ci, c, kt = steps[si]
+            wq = code_pool.tile([P, KT], U32, name="wq", tag="wq", align_bytes=64)
+            ws = code_pool.tile([P, KT], U8, name="ws", tag="ws", align_bytes=64)
+            nc.vector.quantize_mx(
+                out=wq[:].bitcast(E4X4),
+                scales=ws[:],
+                in_=grouped[si][:].rearrange("p w j -> p (w j)"),
+            )
+            codes[(g, c, kt)] = (wq, ws)
+            if last_step[(g, ci, c)] == si:
+                released[(g, ci, c)] = True
+                issue_loads()
+            if (g, 0, kt) in codes and (g, 1, kt) in codes:
+                pend_out.append((g, kt))
+            while pend_out and pend_out[0][0] in grad_ready:
+                og, okt = pend_out.pop(0)
+                outputs(og, okt)
+
+        issue_loads()
+        nc.vector.tensor_copy(out=s_tab[:], in_=s_bf[:].rearrange("p a k -> p (a k)"))
+        grad_transposes(0)
+        ns = len(steps)
+        g1_at = [-1]
+        for si in range(ns + 1):
+            if si == 0:
+                for j in range(LOOK):
+                    if j in S_JOBS:
+                        regroup(j, True)
+            if si + LOOK < ns and (si + LOOK) in S_JOBS:
+                regroup(si + LOOK, True)
+            if g1_at[0] < 0 and 1 in graw and steps[min(si + 4, ns - 1)][0] == 1:
+                grad_transposes(1)
+                g1_at[0] = si + 2
+            if si == GQ0_AT:
+                grad_quantise(0)
+            if si == g1_at[0]:
+                grad_quantise(1)
+            if si < ns and si not in S_JOBS:
+                regroup(si, False)
+            if si >= 1:
+                quantise(si - 1)

@@ -1,8 +1,6 @@
 from contextlib import ExitStack
 
-import concourse.bass as bass
 import concourse.mybir as mybir
-import concourse.tile as tile
 from concourse.masks import make_identity
 
 G, T, K, N = 2, 512, 3584, 1024
@@ -22,33 +20,29 @@ BLK = 128
 NKB = K // BLK
 
 PIN = True
-LOAD_CHUNKS = (((0, 1), (1, 2), (3, 4)), ((0, 4), (4, 3)))
-STORE_CHUNKS = (((0, 3), (3, 4)), ((0, 4), (4, 2), (6, 1)))
-KMAJOR_FROM = 3
-RAW_BUFS = 4
-STAGE_BUFS = 4
+LOAD_CHUNKS = (((0, 1), (1, 2), (3, 4)), ((0, 7),))
+PHASES = (((0, 1, False), (1, 2, False), (3, 4, False)), ((0, 4, False), (4, 3, True)))
+STORE_CHUNKS = (((0, 7, 1),), ((0, 4, 2), (4, 2, 4), (6, 1, 4)))
+BIG_BUFS = 6
 CODE_BUFS = 12
 GRP_BUFS = 3
-S_JOBS = ()
-LOOK = 3
 GRAD_POS = (3, 6)
+GT0_AT = 0
 GQ0_AT = 5
 
 
 def tile_groupcolumnparallellineardeepseekv3_kernel(tc, xs, weight, scale, bias, grad_out, out):
     nc = tc.nc
     mult = mybir.AluOpType.mult
-    copy_fn = mybir.ActivationFunctionType.Copy
 
     with ExitStack() as ctx:
         const = ctx.enter_context(tc.tile_pool(name="const", bufs=1))
         graw_pool = ctx.enter_context(tc.tile_pool(name="graw", bufs=2))
         ggrp_pool = ctx.enter_context(tc.tile_pool(name="ggrp", bufs=2))
-        raw_pool = ctx.enter_context(tc.tile_pool(name="raw", bufs=RAW_BUFS))
+        big_pool = ctx.enter_context(tc.tile_pool(name="big", bufs=BIG_BUFS))
+        row_pool = ctx.enter_context(tc.tile_pool(name="row", bufs=2))
         grp_pool = ctx.enter_context(tc.tile_pool(name="grp", bufs=GRP_BUFS))
-        grps_pool = ctx.enter_context(tc.tile_pool(name="grps", bufs=2))
         code_pool = ctx.enter_context(tc.tile_pool(name="code", bufs=CODE_BUFS))
-        stage_pool = ctx.enter_context(tc.tile_pool(name="stage", bufs=STAGE_BUFS))
         psum = ctx.enter_context(tc.psum_pool(name="psum", bufs=8))
         if PIN:
             ctx.enter_context(tc.manual_schedule())
@@ -56,7 +50,7 @@ def tile_groupcolumnparallellineardeepseekv3_kernel(tc, xs, weight, scale, bias,
         s_bf = const.tile([P, 4, NKB], BF16, name="s_bf", tag="s_bf")
         sview = scale.rearrange("g (c q) k -> (g c) q k", q=4)
         for q in range(4):
-            nc.scalar.dma_start(out=s_bf[32 * q:32 * q + 32, :, :], in_=sview[:, q, :].partition_broadcast(32))
+            nc.sync.dma_start(out=s_bf[32 * q:32 * q + 32, :, :], in_=sview[:, q, :].partition_broadcast(32))
         s_tab = const.tile([P, 4 * NKB], F32, name="s_tab", tag="s_tab")
         ident = const.tile([P, P], F32, name="ident", tag="ident")
         make_identity(nc, ident[:])
@@ -69,32 +63,24 @@ def tile_groupcolumnparallellineardeepseekv3_kernel(tc, xs, weight, scale, bias,
             gq.append(gq_t)
             gs.append(gs_t)
 
-        ltiles = []
         steps = []
         for g in range(G):
-            for ci, (k0, n) in enumerate(LOAD_CHUNKS[g]):
-                chunk_no = len(ltiles) // 2
-                for c in range(2):
-                    ltiles.append((g, ci, c))
-                if chunk_no >= KMAJOR_FROM:
+            for (k0, n, kmajor) in PHASES[g]:
+                if kmajor:
                     for kt in range(k0, k0 + n):
                         for c in range(2):
-                            steps.append((g, ci, c, kt))
+                            steps.append((g, c, kt))
                 else:
                     for c in range(2):
                         for kt in range(k0, k0 + n):
-                            steps.append((g, ci, c, kt))
-        last_step = {}
-        for si, (g, ci, c, kt) in enumerate(steps):
-            last_step[(g, ci, c)] = si
+                            steps.append((g, c, kt))
         sch_of = {}
         for g in range(G):
-            for (k0, n) in STORE_CHUNKS[g]:
+            for (k0, n, ntt) in STORE_CHUNKS[g]:
                 for kt in range(k0, k0 + n):
-                    sch_of[(g, kt)] = (k0, n)
+                    sch_of[(g, kt)] = (k0, n, ntt)
 
         raw = {}
-        released = {}
         graw = {}
         ggrp = {}
         grad_ready = {}
@@ -102,28 +88,28 @@ def tile_groupcolumnparallellineardeepseekv3_kernel(tc, xs, weight, scale, bias,
         codes = {}
         stage = {}
         pend_out = []
-        n_loaded = [0]
 
-        def issue_loads():
-            while n_loaded[0] < len(ltiles):
-                i = n_loaded[0]
-                if i >= RAW_BUFS and ltiles[i - RAW_BUFS] not in released:
-                    return
-                for g in range(G):
-                    if GRAD_POS[g] == i:
-                        gr = graw_pool.tile([P, 4 * N], BF16, name="graw", tag="graw")
-                        nc.sync.dma_start(out=gr[:], in_=grad_out[g].rearrange("(p t) n -> p (t n)", t=4))
-                        graw[g] = gr
-                g, ci, c = ltiles[i]
-                k0, n = LOAD_CHUNKS[g][ci]
-                w = n * KT
-                rt = raw_pool.tile([P, 4, w], BF16, name="raw", tag="raw")
-                nc.sync.dma_start(
-                    out=rt[:],
-                    in_=weight[g, 512 * c:512 * (c + 1), k0 * KT:k0 * KT + w].rearrange("(p j) k -> p j k", j=4),
-                )
-                raw[ltiles[i]] = rt
-                n_loaded[0] += 1
+        n_loads = 0
+        for g in range(G):
+            for (k0, n) in LOAD_CHUNKS[g]:
+                for c in range(2):
+                    for gg in range(G):
+                        if GRAD_POS[gg] == n_loads:
+                            gr = graw_pool.tile([P, 4 * N], BF16, name="graw", tag="graw")
+                            nc.sync.dma_start(out=gr[:], in_=grad_out[gg].rearrange("(p t) n -> p (t n)", t=4))
+                            graw[gg] = gr
+                    w = n * KT
+                    if n == 7:
+                        rt = row_pool.tile([P, 4, w], BF16, name="row", tag="row")
+                    else:
+                        rt = big_pool.tile([P, 4, w], BF16, name="big", tag="big")
+                    nc.sync.dma_start(
+                        out=rt[:],
+                        in_=weight[g, 512 * c:512 * (c + 1), k0 * KT:k0 * KT + w].rearrange("(p j) k -> p j k", j=4),
+                    )
+                    for kt in range(k0, k0 + n):
+                        raw[(g, c, kt)] = (rt, k0)
+                    n_loads += 1
 
         def grad_transposes(g):
             g32 = graw[g][:].bitcast(F32)
@@ -155,59 +141,49 @@ def tile_groupcolumnparallellineardeepseekv3_kernel(tc, xs, weight, scale, bias,
                 )
             grad_ready[g] = True
 
-        def regroup(si, on_scalar):
-            g, ci, c, kt = steps[si]
-            k0, n = LOAD_CHUNKS[g][ci]
-            rt = raw[(g, ci, c)]
-            if on_scalar:
-                gt = grps_pool.tile([P, KT, 4], BF16, name="grps", tag="grps", align_bytes=64)
-            else:
-                gt = grp_pool.tile([P, KT, 4], BF16, name="grp", tag="grp", align_bytes=64)
+        def regroup(si):
+            g, c, kt = steps[si]
+            rt, k0 = raw[(g, c, kt)]
+            gt = grp_pool.tile([P, KT, 4], BF16, name="grp", tag="grp", align_bytes=64)
             grouped[si] = gt
             for b in range(4):
                 x = (kt - k0) * KT + b * BLK
                 col = (2 * g + c) * NKB + 4 * kt + b
                 src = rt[:, :, x:x + BLK].rearrange("p t (c i) -> p c t i", i=4)
                 dst = gt[:, b * BLK:(b + 1) * BLK, :].rearrange("p (c i) t -> p c t i", i=4)
-                if on_scalar:
-                    nc.scalar.activation(out=dst, in_=src, func=copy_fn, scale=s_tab[:, col:col + 1])
-                else:
-                    nc.vector.tensor_scalar(out=dst, in0=src, scalar1=s_tab[:, col:col + 1], scalar2=None, op0=mult)
+                nc.vector.tensor_scalar(out=dst, in0=src, scalar1=s_tab[:, col:col + 1], scalar2=None, op0=mult)
 
         def outputs(g, kt):
-            k0, n = sch_of[(g, kt)]
-            groups = ((0, 1), (2, 3)) if n > 2 else ((0, 1, 2, 3),)
-            for tts in groups:
-                if (g, k0, tts[0]) not in stage:
-                    st = stage_pool.tile([P, len(tts), n * KT], F32, name="st", tag="st")
-                    stage[(g, k0, tts[0])] = st
-            for tts in groups:
-                st = stage[(g, k0, tts[0])]
-                for tl, tt in enumerate(tts):
-                    ps = psum.tile([P, KT], F32, name="ps", tag="ps")
-                    for c in range(2):
-                        wq, ws = codes[(g, c, kt)]
-                        nc.tensor.matmul_mx(
-                            out=ps[:],
-                            lhsT=gq[g][:, c, tt * P:(tt + 1) * P].bitcast(E5X4),
-                            lhsT_scale=gs[g][:, c, tt * P:(tt + 1) * P],
-                            rhs=wq[:].bitcast(E4X4),
-                            rhs_scale=ws[:],
-                            start=(c == 0),
-                            stop=(c == 1),
-                        )
-                    nc.scalar.copy(out=st[:, tl, (kt - k0) * KT:(kt - k0 + 1) * KT], in_=ps[:])
+            k0, n, ntt = sch_of[(g, kt)]
+            for t0 in range(0, 4, ntt):
+                if (g, k0, t0) not in stage:
+                    st = big_pool.tile([P, ntt, n * KT], F32, name="big", tag="big")
+                    stage[(g, k0, t0)] = st
+            for tt in range(4):
+                st = stage[(g, k0, tt - tt % ntt)]
+                ps = psum.tile([P, KT], F32, name="ps", tag="ps")
+                for c in range(2):
+                    wq, ws = codes[(g, c, kt)]
+                    nc.tensor.matmul_mx(
+                        out=ps[:],
+                        lhsT=gq[g][:, c, tt * P:(tt + 1) * P].bitcast(E5X4),
+                        lhsT_scale=gs[g][:, c, tt * P:(tt + 1) * P],
+                        rhs=wq[:].bitcast(E4X4),
+                        rhs_scale=ws[:],
+                        start=(c == 0),
+                        stop=(c == 1),
+                    )
+                nc.scalar.copy(out=st[:, tt % ntt, (kt - k0) * KT:(kt - k0 + 1) * KT], in_=ps[:])
             if kt == k0 + n - 1:
                 oview = out[g].rearrange("(p t) k -> p t k", t=4)
-                for tts in groups:
-                    st = stage[(g, k0, tts[0])]
+                for t0 in range(0, 4, ntt):
                     nc.sync.dma_start(
-                        out=oview[:, tts[0]:tts[0] + len(tts), k0 * KT:(k0 + n) * KT],
-                        in_=st[:],
+                        out=oview[:, t0:t0 + ntt, k0 * KT:(k0 + n) * KT],
+                        in_=stage[(g, k0, t0)][:],
                     )
 
         def quantise(si):
-            g, ci, c, kt = steps[si]
+            g, c, kt = steps[si]
             wq = code_pool.tile([P, KT], U32, name="wq", tag="wq", align_bytes=64)
             ws = code_pool.tile([P, KT], U8, name="ws", tag="ws", align_bytes=64)
             nc.vector.quantize_mx(
@@ -216,35 +192,26 @@ def tile_groupcolumnparallellineardeepseekv3_kernel(tc, xs, weight, scale, bias,
                 in_=grouped[si][:].rearrange("p w j -> p (w j)"),
             )
             codes[(g, c, kt)] = (wq, ws)
-            if last_step[(g, ci, c)] == si:
-                released[(g, ci, c)] = True
-                issue_loads()
             if (g, 0, kt) in codes and (g, 1, kt) in codes:
                 pend_out.append((g, kt))
             while pend_out and pend_out[0][0] in grad_ready:
                 og, okt = pend_out.pop(0)
                 outputs(og, okt)
 
-        issue_loads()
         nc.vector.tensor_copy(out=s_tab[:], in_=s_bf[:].rearrange("p a k -> p (a k)"))
-        grad_transposes(0)
         ns = len(steps)
         g1_at = [-1]
         for si in range(ns + 1):
-            if si == 0:
-                for j in range(LOOK):
-                    if j in S_JOBS:
-                        regroup(j, True)
-            if si + LOOK < ns and (si + LOOK) in S_JOBS:
-                regroup(si + LOOK, True)
-            if g1_at[0] < 0 and 1 in graw and steps[min(si + 4, ns - 1)][0] == 1:
+            if si == GT0_AT:
+                grad_transposes(0)
+            if g1_at[0] < 0 and steps[min(si + 4, ns - 1)][0] == 1:
                 grad_transposes(1)
                 g1_at[0] = si + 2
             if si == GQ0_AT:
                 grad_quantise(0)
             if si == g1_at[0]:
                 grad_quantise(1)
-            if si < ns and si not in S_JOBS:
-                regroup(si, False)
+            if si < ns:
+                regroup(si)
             if si >= 1:
                 quantise(si - 1)

@@ -22,10 +22,11 @@ NKB = K // BLK
 PIN = True
 LOAD_CHUNKS = (((0, 1), (1, 2), (3, 4)), ((0, 7),))
 PHASES = (((0, 1, False), (1, 2, False), (3, 4, False)), ((0, 4, False), (4, 3, True)))
-STORE_CHUNKS = (((0, 7, 1),), ((0, 4, 2), (4, 2, 4), (6, 1, 4)))
+STORE_CHUNKS = (((0, 3, 2), (3, 4, 2)), ((0, 2, 4), (2, 2, 4), (4, 2, 4), (6, 1, 4)))
 BIG_BUFS = 6
-CODE_BUFS = 12
-GRP_BUFS = 3
+CODE_BUFS = 10
+GRP_BUFS = 4
+LOOK = 2
 GRAD_POS = (3, 6)
 GT0_AT = 0
 GQ0_AT = 5
@@ -34,6 +35,7 @@ GQ0_AT = 5
 def tile_groupcolumnparallellineardeepseekv3_kernel(tc, xs, weight, scale, bias, grad_out, out):
     nc = tc.nc
     mult = mybir.AluOpType.mult
+    copy_fn = mybir.ActivationFunctionType.Copy
 
     with ExitStack() as ctx:
         const = ctx.enter_context(tc.tile_pool(name="const", bufs=1))
@@ -141,17 +143,27 @@ def tile_groupcolumnparallellineardeepseekv3_kernel(tc, xs, weight, scale, bias,
                 )
             grad_ready[g] = True
 
-        def regroup(si):
+        def scalar_blocks(si):
+            return 1 if si % 3 else 0
+
+        def regroup(si, on_scalar):
             g, c, kt = steps[si]
             rt, k0 = raw[(g, c, kt)]
-            gt = grp_pool.tile([P, KT, 4], BF16, name="grp", tag="grp", align_bytes=64)
-            grouped[si] = gt
+            if on_scalar:
+                gt = grp_pool.tile([P, KT, 4], BF16, name="grp", tag="grp", align_bytes=64)
+                grouped[si] = gt
+            gt = grouped[si]
+            first_scalar = 4 - scalar_blocks(si)
             for b in range(4):
-                x = (kt - k0) * KT + b * BLK
-                col = (2 * g + c) * NKB + 4 * kt + b
-                src = rt[:, :, x:x + BLK].rearrange("p t (c i) -> p c t i", i=4)
-                dst = gt[:, b * BLK:(b + 1) * BLK, :].rearrange("p (c i) t -> p c t i", i=4)
-                nc.vector.tensor_scalar(out=dst, in0=src, scalar1=s_tab[:, col:col + 1], scalar2=None, op0=mult)
+                if (b >= first_scalar) == on_scalar:
+                    x = (kt - k0) * KT + b * BLK
+                    col = (2 * g + c) * NKB + 4 * kt + b
+                    src = rt[:, :, x:x + BLK].rearrange("p t (c i) -> p c t i", i=4)
+                    dst = gt[:, b * BLK:(b + 1) * BLK, :].rearrange("p (c i) t -> p c t i", i=4)
+                    if on_scalar:
+                        nc.scalar.activation(out=dst, in_=src, func=copy_fn, scale=s_tab[:, col:col + 1])
+                    else:
+                        nc.vector.tensor_scalar(out=dst, in0=src, scalar1=s_tab[:, col:col + 1], scalar2=None, op0=mult)
 
         def outputs(g, kt):
             k0, n, ntt = sch_of[(g, kt)]
@@ -202,6 +214,11 @@ def tile_groupcolumnparallellineardeepseekv3_kernel(tc, xs, weight, scale, bias,
         ns = len(steps)
         g1_at = [-1]
         for si in range(ns + 1):
+            if si == 0:
+                for j in range(LOOK):
+                    regroup(j, True)
+            if si + LOOK < ns:
+                regroup(si + LOOK, True)
             if si == GT0_AT:
                 grad_transposes(0)
             if g1_at[0] < 0 and steps[min(si + 4, ns - 1)][0] == 1:
@@ -212,6 +229,6 @@ def tile_groupcolumnparallellineardeepseekv3_kernel(tc, xs, weight, scale, bias,
             if si == g1_at[0]:
                 grad_quantise(1)
             if si < ns:
-                regroup(si)
+                regroup(si, False)
             if si >= 1:
                 quantise(si - 1)

@@ -20,16 +20,16 @@ BLK = 128
 NKB = K // BLK
 
 PIN = True
-LOAD_CHUNKS = (((0, 1), (1, 2), (3, 4)), ((0, 7),))
-PHASES = (((0, 1, False), (1, 2, False), (3, 4, False)), ((0, 4, False), (4, 3, True)))
+LOAD_CHUNKS = (((0, 3), (3, 4)), ((0, 7),))
+PHASES = (((0, 3, False), (3, 4, False)), ((0, 4, False), (4, 3, True)))
 STORE_CHUNKS = (((0, 3, 2), (3, 4, 2)), ((0, 2, 4), (2, 2, 4), (4, 2, 4), (6, 1, 4)))
 BIG_BUFS = 6
 CODE_BUFS = 10
 GRP_BUFS = 4
 LOOK = 2
-GRAD_POS = (3, 6)
+GRAD_POS = (1, 4)
 GT0_AT = 0
-GQ0_AT = 5
+GQ0_AT = 4
 
 
 def tile_groupcolumnparallellineardeepseekv3_kernel(tc, xs, weight, scale, bias, grad_out, out):

from contextlib import ExitStack

import concourse.mybir as mybir
from concourse.masks import make_identity

G, T, K, N = 2, 512, 3584, 1024
FLOPS = 2 * G * T * K * N
BYTES = G * N * K * 2 + G * 8 * 28 * 2 + G * T * N * 2 + G * T * K * 4

BF16 = mybir.dt.bfloat16
F32 = mybir.dt.float32
U32 = mybir.dt.uint32
U8 = mybir.dt.uint8
E4X4 = mybir.dt.float8_e4m3fn_x4
E5X4 = mybir.dt.float8_e5m2_x4

P = 128
KT = 512
BLK = 128
NKB = K // BLK

PIN = True
LOAD_CHUNKS = (((0, 3), (3, 4)), ((0, 7),))
PHASES = (((0, 3, False), (3, 4, False)), ((0, 4, False), (4, 3, True)))
STORE_CHUNKS = (((0, 3, 2), (3, 4, 2)), ((0, 2, 4), (2, 2, 4), (4, 2, 4), (6, 1, 4)))
BIG_BUFS = 6
CODE_BUFS = 10
GRP_BUFS = 4
LOOK = 2
GRAD_POS = (1, 4)
GT0_AT = 0
GQ0_AT = 4


def tile_groupcolumnparallellineardeepseekv3_kernel(tc, xs, weight, scale, bias, grad_out, out):
    nc = tc.nc
    mult = mybir.AluOpType.mult
    copy_fn = mybir.ActivationFunctionType.Copy

    with ExitStack() as ctx:
        const = ctx.enter_context(tc.tile_pool(name="const", bufs=1))
        graw_pool = ctx.enter_context(tc.tile_pool(name="graw", bufs=2))
        ggrp_pool = ctx.enter_context(tc.tile_pool(name="ggrp", bufs=2))
        big_pool = ctx.enter_context(tc.tile_pool(name="big", bufs=BIG_BUFS))
        row_pool = ctx.enter_context(tc.tile_pool(name="row", bufs=2))
        grp_pool = ctx.enter_context(tc.tile_pool(name="grp", bufs=GRP_BUFS))
        code_pool = ctx.enter_context(tc.tile_pool(name="code", bufs=CODE_BUFS))
        psum = ctx.enter_context(tc.psum_pool(name="psum", bufs=8))
        if PIN:
            ctx.enter_context(tc.manual_schedule())

        s_bf = const.tile([P, 4, NKB], BF16, name="s_bf", tag="s_bf")
        sview = scale.rearrange("g (c q) k -> (g c) q k", q=4)
        for q in range(4):
            nc.sync.dma_start(out=s_bf[32 * q:32 * q + 32, :, :], in_=sview[:, q, :].partition_broadcast(32))
        s_tab = const.tile([P, 4 * NKB], F32, name="s_tab", tag="s_tab")
        ident = const.tile([P, P], F32, name="ident", tag="ident")
        make_identity(nc, ident[:])

        gq = []
        gs = []
        for g in range(G):
            gq_t = const.tile([P, 2, T], U32, name="gq%d" % g, tag="gq%d" % g, align_bytes=64)
            gs_t = const.tile([P, 2, T], U8, name="gs%d" % g, tag="gs%d" % g, align_bytes=64)
            gq.append(gq_t)
            gs.append(gs_t)

        steps = []
        for g in range(G):
            for (k0, n, kmajor) in PHASES[g]:
                if kmajor:
                    for kt in range(k0, k0 + n):
                        for c in range(2):
                            steps.append((g, c, kt))
                else:
                    for c in range(2):
                        for kt in range(k0, k0 + n):
                            steps.append((g, c, kt))
        sch_of = {}
        for g in range(G):
            for (k0, n, ntt) in STORE_CHUNKS[g]:
                for kt in range(k0, k0 + n):
                    sch_of[(g, kt)] = (k0, n, ntt)

        raw = {}
        graw = {}
        ggrp = {}
        grad_ready = {}
        grouped = {}
        codes = {}
        stage = {}
        pend_out = []

        n_loads = 0
        for g in range(G):
            for (k0, n) in LOAD_CHUNKS[g]:
                for c in range(2):
                    for gg in range(G):
                        if GRAD_POS[gg] == n_loads:
                            gr = graw_pool.tile([P, 4 * N], BF16, name="graw", tag="graw")
                            nc.sync.dma_start(out=gr[:], in_=grad_out[gg].rearrange("(p t) n -> p (t n)", t=4))
                            graw[gg] = gr
                    w = n * KT
                    if n == 7:
                        rt = row_pool.tile([P, 4, w], BF16, name="row", tag="row")
                    else:
                        rt = big_pool.tile([P, 4, w], BF16, name="big", tag="big")
                    nc.sync.dma_start(
                        out=rt[:],
                        in_=weight[g, 512 * c:512 * (c + 1), k0 * KT:k0 * KT + w].rearrange("(p j) k -> p j k", j=4),
                    )
                    for kt in range(k0, k0 + n):
                        raw[(g, c, kt)] = (rt, k0)
                    n_loads += 1

        def grad_transposes(g):
            g32 = graw[g][:].bitcast(F32)
            for c in range(2):
                gg = ggrp_pool.tile([P, 4 * T], BF16, name="ggrp", tag="ggrp", align_bytes=64)
                ggrp[(g, c)] = gg
                gg32 = gg[:].bitcast(F32)
                for tp in range(2):
                    ps = psum.tile([P, KT], F32, name="ps", tag="ps")
                    for u in range(2):
                        for tl in range(2):
                            base = (2 * tp + tl) * 512 + 256 * c
                            nc.tensor.transpose(
                                out=ps[:, u * 256 + tl * 128:u * 256 + tl * 128 + 128],
                                in_=g32[:, base + u:base + 256:2],
                                identity=ident[:],
                            )
                    nc.scalar.copy(
                        out=gg32[:, tp * 512:tp * 512 + 512].rearrange("p (x u) -> p x u", u=2),
                        in_=ps[:].rearrange("p (u x) -> p x u", u=2),
                    )

        def grad_quantise(g):
            for c in range(2):
                nc.vector.quantize_mx(
                    out=gq[g][:, c, :].bitcast(E5X4),
                    scales=gs[g][:, c, :],
                    in_=ggrp[(g, c)][:],
                )
            grad_ready[g] = True

        def scalar_blocks(si):
            return 1 if si % 3 else 0

        def regroup(si, on_scalar):
            g, c, kt = steps[si]
            rt, k0 = raw[(g, c, kt)]
            if on_scalar:
                gt = grp_pool.tile([P, KT, 4], BF16, name="grp", tag="grp", align_bytes=64)
                grouped[si] = gt
            gt = grouped[si]
            first_scalar = 4 - scalar_blocks(si)
            for b in range(4):
                if (b >= first_scalar) == on_scalar:
                    x = (kt - k0) * KT + b * BLK
                    col = (2 * g + c) * NKB + 4 * kt + b
                    src = rt[:, :, x:x + BLK].rearrange("p t (c i) -> p c t i", i=4)
                    dst = gt[:, b * BLK:(b + 1) * BLK, :].rearrange("p (c i) t -> p c t i", i=4)
                    if on_scalar:
                        nc.scalar.activation(out=dst, in_=src, func=copy_fn, scale=s_tab[:, col:col + 1])
                    else:
                        nc.vector.tensor_scalar(out=dst, in0=src, scalar1=s_tab[:, col:col + 1], scalar2=None, op0=mult)

        def outputs(g, kt):
            k0, n, ntt = sch_of[(g, kt)]
            for t0 in range(0, 4, ntt):
                if (g, k0, t0) not in stage:
                    st = big_pool.tile([P, ntt, n * KT], F32, name="big", tag="big")
                    stage[(g, k0, t0)] = st
            for tt in range(4):
                st = stage[(g, k0, tt - tt % ntt)]
                ps = psum.tile([P, KT], F32, name="ps", tag="ps")
                for c in range(2):
                    wq, ws = codes[(g, c, kt)]
                    nc.tensor.matmul_mx(
                        out=ps[:],
                        lhsT=gq[g][:, c, tt * P:(tt + 1) * P].bitcast(E5X4),
                        lhsT_scale=gs[g][:, c, tt * P:(tt + 1) * P],
                        rhs=wq[:].bitcast(E4X4),
                        rhs_scale=ws[:],
                        start=(c == 0),
                        stop=(c == 1),
                    )
                nc.scalar.copy(out=st[:, tt % ntt, (kt - k0) * KT:(kt - k0 + 1) * KT], in_=ps[:])
            if kt == k0 + n - 1:
                oview = out[g].rearrange("(p t) k -> p t k", t=4)
                for t0 in range(0, 4, ntt):
                    nc.sync.dma_start(
                        out=oview[:, t0:t0 + ntt, k0 * KT:(k0 + n) * KT],
                        in_=stage[(g, k0, t0)][:],
                    )

        def quantise(si):
            g, c, kt = steps[si]
            wq = code_pool.tile([P, KT], U32, name="wq", tag="wq", align_bytes=64)
            ws = code_pool.tile([P, KT], U8, name="ws", tag="ws", align_bytes=64)
            nc.vector.quantize_mx(
                out=wq[:].bitcast(E4X4),
                scales=ws[:],
                in_=grouped[si][:].rearrange("p w j -> p (w j)"),
            )
            codes[(g, c, kt)] = (wq, ws)
            if (g, 0, kt) in codes and (g, 1, kt) in codes:
                pend_out.append((g, kt))
            while pend_out and pend_out[0][0] in grad_ready:
                og, okt = pend_out.pop(0)
                outputs(og, okt)

        nc.vector.tensor_copy(out=s_tab[:], in_=s_bf[:].rearrange("p a k -> p (a k)"))
        ns = len(steps)
        g1_at = [-1]
        for si in range(ns + 1):
            if si == 0:
                for j in range(LOOK):
                    regroup(j, True)
            if si + LOOK < ns:
                regroup(si + LOOK, True)
            if si == GT0_AT:
                grad_transposes(0)
            if g1_at[0] < 0 and steps[min(si + 4, ns - 1)][0] == 1:
                grad_transposes(1)
                g1_at[0] = si + 2
            if si == GQ0_AT:
                grad_quantise(0)
            if si == g1_at[0]:
                grad_quantise(1)
            if si < ns:
                regroup(si, False)
            if si >= 1:
                quantise(si - 1)
